import numpy as np
import ml_dtypes


def mxq(x, axis, fmt="e4m3"):
    dtype, down = {"e4m3": (ml_dtypes.float8_e4m3fn, 7), "e5m2": (ml_dtypes.float8_e5m2, 14)}[fmt]
    v = np.moveaxis(np.asarray(x, np.float32).astype(ml_dtypes.bfloat16).astype(np.float64), axis, -1)
    blocks = v.reshape(v.shape[:-1] + (-1, 32))
    amax = np.abs(blocks).max(-1, keepdims=True)
    byte = np.maximum(np.where(amax > 0, np.frexp(amax)[1] - 1 + 127, 0) - down, 1)
    scale = np.exp2(byte - 127.0)
    codes = (blocks / scale).astype(np.float32).astype(dtype).astype(np.float64)
    return np.moveaxis((codes * scale).reshape(v.shape), -1, axis)


WIDE = False


def mx_kscale(k):
    if not WIDE:
        return np.ones(k)
    levels = np.array([20, -20, 10, -10, 0])
    a = np.random.permutation(np.resize(levels, k // 512 * 4)).reshape(k // 512, 4)
    idx = np.arange(k)
    return np.exp2(a[idx // 512, idx % 128 // 32])


BF16 = ml_dtypes.bfloat16


def bf(x):
    return np.asarray(x, np.float32).astype(BF16)


def f64(x):
    return np.asarray(x).astype(np.float64)


M, K, N = 8192, 512, 512


def setup_inputs():
    u = mx_kscale(N)
    A = np.random.standard_normal((M, K))
    B = np.random.standard_normal((K, N)) * 2.0 / np.sqrt(K) / u[None, :]
    g = np.random.standard_normal((M, N)) * np.exp2(np.random.randint(-12, 1, (M, 1))) * 4.0 * u[None, :]
    return {"A": bf(A), "B": bf(B), "grad_out": bf(g)}


def reference(A, B, grad_out):
    G = np.tril(f64(grad_out))
    L = np.tril(f64(B))
    gA = mxq(G, 1, "e5m2") @ mxq(L, 1, "e4m3").T
    return np.tril(gA)

@@ -1,0 +1,187 @@
+from contextlib import ExitStack
+
+import concourse.mybir as mybir
+from concourse.masks import make_identity
+
+F32 = mybir.dt.float32
+BF16 = mybir.dt.bfloat16
+U32 = mybir.dt.uint32
+U8 = mybir.dt.uint8
+E4M3X4 = mybir.dt.float8_e4m3fn_x4
+E5M2X4 = mybir.dt.float8_e5m2_x4
+IS_GE = mybir.AluOpType.is_ge
+
+P = 128
+M, K, N = 8192, 512, 512
+FLOPS = 2 * M * K * N
+BYTES = M * N * 2 + K * N * 2 + M * K * 4
+
+GROUP = 4
+HEAD_TILES = 4
+REST_TILES = M // P - HEAD_TILES
+LOAD_TILES = [4, 8, 12, 12, 12, 12]
+STORE_TILES = [8, 8, 8, 8, 8, 8, 8, 4]
+assert sum(LOAD_TILES) == REST_TILES
+assert sum(STORE_TILES) == REST_TILES
+
+
+def tile_modelnew_t_kernel(tc, A, B, grad_out, out):
+    nc = tc.nc
+    with ExitStack() as ctx:
+        consts = ctx.enter_context(tc.tile_pool(name="consts", bufs=1))
+        resident = ctx.enter_context(tc.tile_pool(name="resident", bufs=1))
+        work = ctx.enter_context(tc.tile_pool(name="work", bufs=3))
+        staging = ctx.enter_context(tc.tile_pool(name="staging", bufs=6))
+        tpsum = ctx.enter_context(tc.psum_pool(name="tpsum", bufs=4))
+        apsum = ctx.enter_context(tc.psum_pool(name="apsum", bufs=4))
+
+        b_sb = resident.tile([P, HEAD_TILES, N], BF16, name="b_sb")
+        nc.sync.dma_start(out=b_sb[:], in_=B.rearrange("(t p) n -> p t n", p=P))
+        g_head = resident.tile([P, HEAD_TILES, N], BF16, name="g_head")
+        nc.sync.dma_start(
+            out=g_head[:], in_=grad_out[0 : HEAD_TILES * P, :].rearrange("(t p) n -> p t n", p=P)
+        )
+        g_rest = grad_out[HEAD_TILES * P : M, :].rearrange("(p t) n -> p t n", t=REST_TILES)
+        o_rest = out[HEAD_TILES * P : M, :].rearrange("(p t) k -> p t k", t=REST_TILES)
+        row_tiles = [g_head[:, t, :] for t in range(HEAD_TILES)]
+        first = 0
+        for c, count in enumerate(LOAD_TILES):
+            chunk = resident.tile([P, count, N], BF16, name="g_chunk%d" % c)
+            nc.sync.dma_start(out=chunk[:], in_=g_rest[:, first : first + count, :])
+            row_tiles.extend([chunk[:, t, :] for t in range(count)])
+            first += count
+
+        ident = consts.tile([P, P], F32, name="ident")
+        make_identity(nc, ident[:])
+
+        diag = consts.tile([P, 2 * HEAD_TILES, P], F32, name="diag")
+
+        def mask_lower(src, half):
+            cut = diag[:, half * HEAD_TILES : (half + 1) * HEAD_TILES, :]
+            for t in range(HEAD_TILES):
+                nc.vector.tensor_copy(out=cut[:, t, :], in_=src[:, t, t * P : (t + 1) * P])
+            nc.gpsimd.affine_select(
+                out=cut,
+                in_=cut,
+                pattern=[[0, HEAD_TILES], [-1, P]],
+                compare_op=IS_GE,
+                fill=0.0,
+                base=0,
+                channel_multiplier=1,
+            )
+            for t in range(HEAD_TILES):
+                nc.vector.tensor_copy(out=src[:, t, t * P : (t + 1) * P], in_=cut[:, t, :])
+                if (t + 1) * P < N:
+                    nc.vector.memset(src[:, t, (t + 1) * P : N], 0.0)
+
+        def transposes(tiles):
+            banks = []
+            for j in range(2):
+                bank = tpsum.tile([P, 512], F32, name="bank")
+                for a in range(2):
+                    words = tiles[2 * j + a].bitcast(F32)
+                    for u in range(2):
+                        col = (2 * a + u) * P
+                        nc.tensor.transpose(
+                            out=bank[:, col : col + P],
+                            in_=words[:, u * P : (u + 1) * P],
+                            identity=ident[:],
+                        )
+                banks.append(bank)
+            return banks
+
+        def regroup(banks, pool, name):
+            grouped = pool.tile([P, GROUP * P * 4], BF16, name=name, align_bytes=64)
+            words = grouped[:].bitcast(F32)
+            for j in range(2):
+                nc.vector.tensor_copy(
+                    out=words[:, 512 * j : 512 * (j + 1)].rearrange(
+                        "p (a m u) -> p a m u", a=2, u=2
+                    ),
+                    in_=banks[j][:].rearrange("p (a u m) -> p a m u", a=2, u=2),
+                )
+            return grouped
+
+        def quantise(grouped, pool, name, fmt):
+            codes = pool.tile([P, GROUP * P], U32, name=name + "_codes", align_bytes=64)
+            scales = pool.tile([P, GROUP * P], U8, name=name + "_scales", align_bytes=64)
+            nc.vector.quantize_mx(out=codes[:].bitcast(fmt), scales=scales[:], in_=grouped[:])
+            return codes, scales
+
+        mask_lower(b_sb, 0)
+        l_banks = transposes([b_sb[:, t, :] for t in range(HEAD_TILES)])
+        l_grouped = regroup(l_banks, consts, "l_grouped")
+        l_codes, l_scales = quantise(l_grouped, consts, "l", E4M3X4)
+        mask_lower(g_head, 1)
+
+        n_groups = (M // P) // GROUP
+        store_of = {0: (0, HEAD_TILES)}
+        first = HEAD_TILES
+        for count in STORE_TILES:
+            for g in range(first // GROUP, (first + count) // GROUP):
+                store_of[g] = (first, count)
+            first += count
+
+        banks_of = {}
+        grouped_of = {}
+        quant_of = {}
+        stage_of = {}
+
+        def do_t(g):
+            banks_of[g] = transposes(row_tiles[g * GROUP : (g + 1) * GROUP])
+
+        def do_c(g):
+            grouped_of[g] = regroup(banks_of[g], work, "grouped")
+
+        def do_q(g):
+            quant_of[g] = quantise(grouped_of[g], work, "g", E5M2X4)
+
+        def do_mx(g):
+            start_tile, count = store_of[g]
+            if g * GROUP == start_tile:
+                stage_of[start_tile] = staging.tile([P, 8, K], F32, name="stage")
+            stage = stage_of[start_tile]
+            codes, scales = quant_of[g]
+            for a in range(GROUP):
+                acc = apsum.tile([P, K], F32, name="acc")
+                nc.tensor.matmul_mx(
+                    out=acc[:],
+                    lhsT=codes[:, a * P : (a + 1) * P].bitcast(E5M2X4),
+                    lhsT_scale=scales[:, a * P : (a + 1) * P],
+                    rhs=l_codes[:].bitcast(E4M3X4),
+                    rhs_scale=l_scales[:],
+                    start=True,
+                    stop=True,
+                )
+                nc.scalar.copy(out=stage[:, g * GROUP + a - start_tile, :], in_=acc[:])
+            if g == 0:
+                nc.gpsimd.affine_select(
+                    out=stage[:, 0:HEAD_TILES, :],
+                    in_=stage[:, 0:HEAD_TILES, :],
+                    pattern=[[P, HEAD_TILES], [-1, K]],
+                    compare_op=IS_GE,
+                    fill=0.0,
+                    base=0,
+                    channel_multiplier=1,
+                )
+                nc.sync.dma_start(
+                    out=out[0 : HEAD_TILES * P, :].rearrange("(t p) k -> p t k", p=P),
+                    in_=stage[:, 0:HEAD_TILES, :],
+                )
+            elif (g + 1) * GROUP == start_tile + count:
+                lo = start_tile - HEAD_TILES
+                nc.sync.dma_start(out=o_rest[:, lo : lo + count, :], in_=stage[:, 0:count, :])
+
+        do_t(0)
+        do_c(0)
+        do_t(1)
+        do_c(1)
+        do_q(0)
+        for g in range(n_groups):
+            if g + 2 < n_groups:
+                do_t(g + 2)
+            do_mx(g)
+            if g + 2 < n_groups:
+                do_c(g + 2)
+            if g + 1 < n_groups:
+                do_q(g + 1)

@@ -19,10 +19,9 @@ BYTES = M * N * 2 + K * N * 2 + M * K * 4
 GROUP = 4
 HEAD_TILES = 4
 REST_TILES = M // P - HEAD_TILES
-LOAD_TILES = [4, 8, 12, 12, 12, 12]
-STORE_TILES = [8, 8, 8, 8, 8, 8, 8, 4]
-assert sum(LOAD_TILES) == REST_TILES
-assert sum(STORE_TILES) == REST_TILES
+LOAD_PLAN = ["B", 4, 8, "head", 12, 12, 12, 12]
+STORE_PLAN = [4, 8, "head", 8, 8, 8, 8, 8, 8]
+STAGE_TILES = 8
 
 
 def tile_modelnew_t_kernel(tc, A, B, grad_out, out):
@@ -35,21 +34,26 @@ def tile_modelnew_t_kernel(tc, A, B, grad_out, out):
         tpsum = ctx.enter_context(tc.psum_pool(name="tpsum", bufs=4))
         apsum = ctx.enter_context(tc.psum_pool(name="apsum", bufs=4))
 
-        b_sb = resident.tile([P, HEAD_TILES, N], BF16, name="b_sb")
-        nc.sync.dma_start(out=b_sb[:], in_=B.rearrange("(t p) n -> p t n", p=P))
-        g_head = resident.tile([P, HEAD_TILES, N], BF16, name="g_head")
-        nc.sync.dma_start(
-            out=g_head[:], in_=grad_out[0 : HEAD_TILES * P, :].rearrange("(t p) n -> p t n", p=P)
-        )
         g_rest = grad_out[HEAD_TILES * P : M, :].rearrange("(p t) n -> p t n", t=REST_TILES)
         o_rest = out[HEAD_TILES * P : M, :].rearrange("(p t) k -> p t k", t=REST_TILES)
-        row_tiles = [g_head[:, t, :] for t in range(HEAD_TILES)]
-        first = 0
-        for c, count in enumerate(LOAD_TILES):
-            chunk = resident.tile([P, count, N], BF16, name="g_chunk%d" % c)
-            nc.sync.dma_start(out=chunk[:], in_=g_rest[:, first : first + count, :])
-            row_tiles.extend([chunk[:, t, :] for t in range(count)])
-            first += count
+        b_sb = resident.tile([P, HEAD_TILES, N], BF16, name="b_sb")
+        g_head = resident.tile([P, HEAD_TILES, N], BF16, name="g_head")
+
+        def load_lower(dst, src):
+            nc.sync.dma_start(out=dst[:], in_=src.rearrange("(t p) n -> p t n", p=P))
+
+        rest_tiles = []
+        for c, item in enumerate(LOAD_PLAN):
+            if item == "B":
+                load_lower(b_sb, B)
+            elif item == "head":
+                load_lower(g_head, grad_out[0 : HEAD_TILES * P, :])
+            else:
+                first = len(rest_tiles)
+                chunk = resident.tile([P, item, N], BF16, name="g_chunk%d" % c)
+                nc.sync.dma_start(out=chunk[:], in_=g_rest[:, first : first + item, :])
+                rest_tiles.extend([chunk[:, t, :] for t in range(item)])
+        assert len(rest_tiles) == REST_TILES
 
         ident = consts.tile([P, P], F32, name="ident")
         make_identity(nc, ident[:])
@@ -114,13 +118,21 @@ def tile_modelnew_t_kernel(tc, A, B, grad_out, out):
         l_codes, l_scales = quantise(l_grouped, consts, "l", E4M3X4)
         mask_lower(g_head, 1)
 
-        n_groups = (M // P) // GROUP
-        store_of = {0: (0, HEAD_TILES)}
-        first = HEAD_TILES
-        for count in STORE_TILES:
-            for g in range(first // GROUP, (first + count) // GROUP):
-                store_of[g] = (first, count)
-            first += count
+        groups = []
+        store_rows = []
+        first = 0
+        for s, item in enumerate(STORE_PLAN):
+            if item == "head":
+                store_rows.append((None, HEAD_TILES))
+                groups.append(([g_head[:, t, :] for t in range(HEAD_TILES)], s, 0, True))
+            else:
+                store_rows.append((first, item))
+                for lo in range(0, item, GROUP):
+                    tiles = rest_tiles[first + lo : first + lo + GROUP]
+                    groups.append((tiles, s, lo, lo + GROUP == item))
+                first += item
+        assert first == REST_TILES
+        n_groups = len(groups)
 
         banks_of = {}
         grouped_of = {}
@@ -128,7 +140,7 @@ def tile_modelnew_t_kernel(tc, A, B, grad_out, out):
         stage_of = {}
 
         def do_t(g):
-            banks_of[g] = transposes(row_tiles[g * GROUP : (g + 1) * GROUP])
+            banks_of[g] = transposes(groups[g][0])
 
         def do_c(g):
             grouped_of[g] = regroup(banks_of[g], work, "grouped")
@@ -137,10 +149,10 @@ def tile_modelnew_t_kernel(tc, A, B, grad_out, out):
             quant_of[g] = quantise(grouped_of[g], work, "g", E5M2X4)
 
         def do_mx(g):
-            start_tile, count = store_of[g]
-            if g * GROUP == start_tile:
-                stage_of[start_tile] = staging.tile([P, 8, K], F32, name="stage")
-            stage = stage_of[start_tile]
+            tiles, s, lo, last = groups[g]
+            if lo == 0:
+                stage_of[s] = staging.tile([P, STAGE_TILES, K], F32, name="stage")
+            stage = stage_of[s]
             codes, scales = quant_of[g]
             for a in range(GROUP):
                 acc = apsum.tile([P, K], F32, name="acc")
@@ -153,24 +165,27 @@ def tile_modelnew_t_kernel(tc, A, B, grad_out, out):
                     start=True,
                     stop=True,
                 )
-                nc.scalar.copy(out=stage[:, g * GROUP + a - start_tile, :], in_=acc[:])
-            if g == 0:
-                nc.gpsimd.affine_select(
-                    out=stage[:, 0:HEAD_TILES, :],
-                    in_=stage[:, 0:HEAD_TILES, :],
-                    pattern=[[P, HEAD_TILES], [-1, K]],
-                    compare_op=IS_GE,
-                    fill=0.0,
-                    base=0,
-                    channel_multiplier=1,
-                )
-                nc.sync.dma_start(
-                    out=out[0 : HEAD_TILES * P, :].rearrange("(t p) k -> p t k", p=P),
-                    in_=stage[:, 0:HEAD_TILES, :],
-                )
-            elif (g + 1) * GROUP == start_tile + count:
-                lo = start_tile - HEAD_TILES
-                nc.sync.dma_start(out=o_rest[:, lo : lo + count, :], in_=stage[:, 0:count, :])
+                nc.scalar.copy(out=stage[:, lo + a, :], in_=acc[:])
+            if last:
+                first_tile, count = store_rows[s]
+                if first_tile is None:
+                    nc.gpsimd.affine_select(
+                        out=stage[:, 0:count, :],
+                        in_=stage[:, 0:count, :],
+                        pattern=[[P, count], [-1, K]],
+                        compare_op=IS_GE,
+                        fill=0.0,
+                        base=0,
+                        channel_multiplier=1,
+                    )
+                    nc.sync.dma_start(
+                        out=out[0 : count * P, :].rearrange("(t p) k -> p t k", p=P),
+                        in_=stage[:, 0:count, :],
+                    )
+                else:
+                    nc.sync.dma_start(
+                        out=o_rest[:, first_tile : first_tile + count, :], in_=stage[:, 0:count, :]
+                    )
 
         do_t(0)
         do_c(0)

@@ -19,9 +19,15 @@ BYTES = M * N * 2 + K * N * 2 + M * K * 4
 GROUP = 4
 HEAD_TILES = 4
 REST_TILES = M // P - HEAD_TILES
-LOAD_PLAN = ["B", 4, 8, "head", 12, 12, 12, 12]
-STORE_PLAN = [4, 8, "head", 8, 8, 8, 8, 8, 8]
+DIAG_STEP = N + P
+LOAD_PLAN = [4, "B", 4, 8, 8, "head", 12, 12, 12]
+STORE_PLAN = [8, 8, 8, "head", 8, 8, 8, 8, 4]
 STAGE_TILES = 8
+AHEAD = 4
+
+
+def diagonal(flat):
+    return flat[:, 0 : HEAD_TILES * DIAG_STEP].rearrange("p (t c) -> p t c", c=DIAG_STEP)[:, :, 0:P]
 
 
 def tile_modelnew_t_kernel(tc, A, B, grad_out, out):
@@ -30,17 +36,26 @@ def tile_modelnew_t_kernel(tc, A, B, grad_out, out):
         consts = ctx.enter_context(tc.tile_pool(name="consts", bufs=1))
         resident = ctx.enter_context(tc.tile_pool(name="resident", bufs=1))
         work = ctx.enter_context(tc.tile_pool(name="work", bufs=3))
+        quant = ctx.enter_context(tc.tile_pool(name="quant", bufs=AHEAD + 1))
         staging = ctx.enter_context(tc.tile_pool(name="staging", bufs=6))
         tpsum = ctx.enter_context(tc.psum_pool(name="tpsum", bufs=4))
         apsum = ctx.enter_context(tc.psum_pool(name="apsum", bufs=4))
+        ctx.enter_context(tc.manual_schedule())
 
         g_rest = grad_out[HEAD_TILES * P : M, :].rearrange("(p t) n -> p t n", t=REST_TILES)
         o_rest = out[HEAD_TILES * P : M, :].rearrange("(p t) k -> p t k", t=REST_TILES)
-        b_sb = resident.tile([P, HEAD_TILES, N], BF16, name="b_sb")
-        g_head = resident.tile([P, HEAD_TILES, N], BF16, name="g_head")
+        b_sb = resident.tile([P, HEAD_TILES * DIAG_STEP], BF16, name="b_sb")
+        g_head = resident.tile([P, HEAD_TILES * DIAG_STEP], BF16, name="g_head")
+
+        def zero_above(eng, flat):
+            for t in range(HEAD_TILES - 1):
+                eng.memset(flat[:, t * N + (t + 1) * P : (t + 1) * N], 0.0)
 
         def load_lower(dst, src):
-            nc.sync.dma_start(out=dst[:], in_=src.rearrange("(t p) n -> p t n", p=P))
+            nc.sync.dma_start(
+                out=dst[:, 0 : HEAD_TILES * N].rearrange("p (t n) -> p t n", n=N),
+                in_=src.rearrange("(t p) n -> p t n", p=P),
+            )
 
         rest_tiles = []
         for c, item in enumerate(LOAD_PLAN):
@@ -58,25 +73,26 @@ def tile_modelnew_t_kernel(tc, A, B, grad_out, out):
         ident = consts.tile([P, P], F32, name="ident")
         make_identity(nc, ident[:])
 
-        diag = consts.tile([P, 2 * HEAD_TILES, P], F32, name="diag")
-
-        def mask_lower(src, half):
-            cut = diag[:, half * HEAD_TILES : (half + 1) * HEAD_TILES, :]
-            for t in range(HEAD_TILES):
-                nc.vector.tensor_copy(out=cut[:, t, :], in_=src[:, t, t * P : (t + 1) * P])
+        def select_lower(blocks):
             nc.gpsimd.affine_select(
-                out=cut,
-                in_=cut,
+                out=blocks,
+                in_=blocks,
                 pattern=[[0, HEAD_TILES], [-1, P]],
                 compare_op=IS_GE,
                 fill=0.0,
                 base=0,
                 channel_multiplier=1,
             )
-            for t in range(HEAD_TILES):
-                nc.vector.tensor_copy(out=src[:, t, t * P : (t + 1) * P], in_=cut[:, t, :])
-                if (t + 1) * P < N:
-                    nc.vector.memset(src[:, t, (t + 1) * P : N], 0.0)
+
+        def mask_begin(flat, name):
+            wide = consts.tile([P, HEAD_TILES, P], F32, name=name)
+            nc.vector.tensor_copy(out=wide[:], in_=diagonal(flat))
+            select_lower(wide[:])
+            zero_above(nc.vector, flat)
+            return wide
+
+        def mask_end(flat, wide):
+            nc.vector.tensor_copy(out=diagonal(flat), in_=wide[:])
 
         def transposes(tiles):
             banks = []
@@ -98,12 +114,12 @@ def tile_modelnew_t_kernel(tc, A, B, grad_out, out):
             grouped = pool.tile([P, GROUP * P * 4], BF16, name=name, align_bytes=64)
             words = grouped[:].bitcast(F32)
             for j in range(2):
-                nc.vector.tensor_copy(
-                    out=words[:, 512 * j : 512 * (j + 1)].rearrange(
-                        "p (a m u) -> p a m u", a=2, u=2
-                    ),
-                    in_=banks[j][:].rearrange("p (a u m) -> p a m u", a=2, u=2),
-                )
+                dst = words[:, 512 * j : 512 * (j + 1)].rearrange("p (a m u) -> p a m u", a=2, u=2)
+                src = banks[j][:].rearrange("p (a u m) -> p a m u", a=2, u=2)
+                if j == 0:
+                    nc.vector.tensor_copy(out=dst, in_=src)
+                else:
+                    nc.scalar.copy(out=dst, in_=src)
             return grouped
 
         def quantise(grouped, pool, name, fmt):
@@ -112,11 +128,6 @@ def tile_modelnew_t_kernel(tc, A, B, grad_out, out):
             nc.vector.quantize_mx(out=codes[:].bitcast(fmt), scales=scales[:], in_=grouped[:])
             return codes, scales
 
-        mask_lower(b_sb, 0)
-        l_banks = transposes([b_sb[:, t, :] for t in range(HEAD_TILES)])
-        l_grouped = regroup(l_banks, consts, "l_grouped")
-        l_codes, l_scales = quantise(l_grouped, consts, "l", E4M3X4)
-        mask_lower(g_head, 1)
 
         groups = []
         store_rows = []
@@ -124,7 +135,7 @@ def tile_modelnew_t_kernel(tc, A, B, grad_out, out):
         for s, item in enumerate(STORE_PLAN):
             if item == "head":
                 store_rows.append((None, HEAD_TILES))
-                groups.append(([g_head[:, t, :] for t in range(HEAD_TILES)], s, 0, True))
+                groups.append((None, s, 0, True))
             else:
                 store_rows.append((first, item))
                 for lo in range(0, item, GROUP):
@@ -140,13 +151,16 @@ def tile_modelnew_t_kernel(tc, A, B, grad_out, out):
         stage_of = {}
 
         def do_t(g):
-            banks_of[g] = transposes(groups[g][0])
+            tiles = groups[g][0]
+            if tiles is None:
+                tiles = [g_head[:, t * N : (t + 1) * N] for t in range(HEAD_TILES)]
+            banks_of[g] = transposes(tiles)
 
         def do_c(g):
             grouped_of[g] = regroup(banks_of[g], work, "grouped")
 
         def do_q(g):
-            quant_of[g] = quantise(grouped_of[g], work, "g", E5M2X4)
+            quant_of[g] = quantise(grouped_of[g], quant, "g", E5M2X4)
 
         def do_mx(g):
             tiles, s, lo, last = groups[g]
@@ -165,7 +179,10 @@ def tile_modelnew_t_kernel(tc, A, B, grad_out, out):
                     start=True,
                     stop=True,
                 )
-                nc.scalar.copy(out=stage[:, lo + a, :], in_=acc[:])
+                if ((g * GROUP + a) * 1) % 3 < 1:
+                    nc.vector.tensor_copy(out=stage[:, lo + a, :], in_=acc[:])
+                else:
+                    nc.scalar.copy(out=stage[:, lo + a, :], in_=acc[:])
             if last:
                 first_tile, count = store_rows[s]
                 if first_tile is None:
@@ -187,16 +204,36 @@ def tile_modelnew_t_kernel(tc, A, B, grad_out, out):
                         out=o_rest[:, first_tile : first_tile + count, :], in_=stage[:, 0:count, :]
                     )
 
-        do_t(0)
+        head_at = [g for g in range(n_groups) if groups[g][0] is None][0]
+        wide_of = {}
+
+        def flip(g):
+            if g + 2 == head_at:
+                wide_of[0] = mask_begin(g_head, "g_diag")
+            if g + 1 == head_at:
+                mask_end(g_head, wide_of[0])
+            do_t(g)
+
+        flip(0)
+        b_wide = mask_begin(b_sb, "b_diag")
         do_c(0)
-        do_t(1)
+        mask_end(b_sb, b_wide)
+        flip(1)
+        l_banks = transposes([b_sb[:, t * N : (t + 1) * N] for t in range(HEAD_TILES)])
         do_c(1)
+        l_grouped = regroup(l_banks, consts, "l_grouped")
+        l_codes, l_scales = quantise(l_grouped, consts, "l", E4M3X4)
         do_q(0)
+        for g in range(2, AHEAD + 1):
+            flip(g)
+            if g < AHEAD:
+                do_c(g)
+                do_q(g - 1)
         for g in range(n_groups):
-            if g + 2 < n_groups:
-                do_t(g + 2)
+            if g + AHEAD + 1 < n_groups:
+                flip(g + AHEAD + 1)
+            if g + AHEAD < n_groups:
+                do_c(g + AHEAD)
+            if g + AHEAD - 1 < n_groups:
+                do_q(g + AHEAD - 1)
             do_mx(g)
-            if g + 2 < n_groups:
-                do_c(g + 2)
-            if g + 1 < n_groups:
-                do_q(g + 1)

@@ -52,10 +52,12 @@ def tile_modelnew_t_kernel(tc, A, B, grad_out, out):
                 eng.memset(flat[:, t * N + (t + 1) * P : (t + 1) * N], 0.0)
 
         def load_lower(dst, src):
-            nc.sync.dma_start(
-                out=dst[:, 0 : HEAD_TILES * N].rearrange("p (t n) -> p t n", n=N),
-                in_=src.rearrange("(t p) n -> p t n", p=P),
-            )
+            zero_above(nc.vector, dst)
+            for t in range(HEAD_TILES):
+                kept = (t + 1) * P
+                nc.sync.dma_start(
+                    out=dst[:, t * N : t * N + kept], in_=src[t * P : (t + 1) * P, 0:kept]
+                )
 
         rest_tiles = []
         for c, item in enumerate(LOAD_PLAN):
@@ -88,7 +90,6 @@ def tile_modelnew_t_kernel(tc, A, B, grad_out, out):
             wide = consts.tile([P, HEAD_TILES, P], F32, name=name)
             nc.vector.tensor_copy(out=wide[:], in_=diagonal(flat))
             select_lower(wide[:])
-            zero_above(nc.vector, flat)
             return wide
 
         def mask_end(flat, wide):

@@ -21,9 +21,9 @@ HEAD_TILES = 4
 REST_TILES = M // P - HEAD_TILES
 DIAG_STEP = N + P
 LOAD_PLAN = [4, "B", 4, 8, 8, "head", 12, 12, 12]
-STORE_PLAN = [8, 8, 8, "head", 8, 8, 8, 8, 4]
+STORE_PLAN = [8, 8, 8, 8, "head", 8, 8, 8, 4]
 STAGE_TILES = 8
-AHEAD = 4
+AHEAD = 2
 
 
 def diagonal(flat):
@@ -184,18 +184,19 @@ def tile_modelnew_t_kernel(tc, A, B, grad_out, out):
                     nc.vector.tensor_copy(out=stage[:, lo + a, :], in_=acc[:])
                 else:
                     nc.scalar.copy(out=stage[:, lo + a, :], in_=acc[:])
-            if last:
-                first_tile, count = store_rows[s]
-                if first_tile is None:
+                if tiles is None:
                     nc.gpsimd.affine_select(
-                        out=stage[:, 0:count, :],
-                        in_=stage[:, 0:count, :],
-                        pattern=[[P, count], [-1, K]],
+                        out=stage[:, a, a * P : K],
+                        in_=stage[:, a, a * P : K],
+                        pattern=[[-1, K - a * P]],
                         compare_op=IS_GE,
                         fill=0.0,
                         base=0,
                         channel_multiplier=1,
                     )
+            if last:
+                first_tile, count = store_rows[s]
+                if first_tile is None:
                     nc.sync.dma_start(
                         out=out[0 : count * P, :].rearrange("(t p) k -> p t k", p=P),
                         in_=stage[:, 0:count, :],

@@ -105,7 +105,7 @@ def tile_modelnew_t_kernel(tc, A, B, grad_out, out):
                         col = (2 * a + u) * P
                         nc.tensor.transpose(
                             out=bank[:, col : col + P],
-                            in_=words[:, u * P : (u + 1) * P],
+                            in_=words[:, u : 2 * P : 2],
                             identity=ident[:],
                         )
                 banks.append(bank)

@@ -44,8 +44,8 @@ def tile_modelnew_t_kernel(tc, A, B, grad_out, out):
 
         g_rest = grad_out[HEAD_TILES * P : M, :].rearrange("(p t) n -> p t n", t=REST_TILES)
         o_rest = out[HEAD_TILES * P : M, :].rearrange("(p t) k -> p t k", t=REST_TILES)
-        b_sb = resident.tile([P, HEAD_TILES * DIAG_STEP], BF16, name="b_sb")
-        g_head = resident.tile([P, HEAD_TILES * DIAG_STEP], BF16, name="g_head")
+        b_sb = resident.tile([P, HEAD_TILES * DIAG_STEP], BF16, name="b_sb", align_bytes=256)
+        g_head = resident.tile([P, HEAD_TILES * DIAG_STEP], BF16, name="g_head", align_bytes=256)
 
         def zero_above(eng, flat):
             for t in range(HEAD_TILES - 1):
@@ -67,7 +67,7 @@ def tile_modelnew_t_kernel(tc, A, B, grad_out, out):
                 load_lower(g_head, grad_out[0 : HEAD_TILES * P, :])
             else:
                 first = len(rest_tiles)
-                chunk = resident.tile([P, item, N], BF16, name="g_chunk%d" % c)
+                chunk = resident.tile([P, item, N], BF16, name="g_chunk%d" % c, align_bytes=256)
                 nc.sync.dma_start(out=chunk[:], in_=g_rest[:, first : first + item, :])
                 rest_tiles.extend([chunk[:, t, :] for t in range(item)])
         assert len(rest_tiles) == REST_TILES
@@ -166,7 +166,7 @@ def tile_modelnew_t_kernel(tc, A, B, grad_out, out):
         def do_mx(g):
             tiles, s, lo, last = groups[g]
             if lo == 0:
-                stage_of[s] = staging.tile([P, STAGE_TILES, K], F32, name="stage")
+                stage_of[s] = staging.tile([P, STAGE_TILES, K], F32, name="stage", align_bytes=256)
             stage = stage_of[s]
             codes, scales = quant_of[g]
             for a in range(GROUP):

@@ -20,9 +20,8 @@ GROUP = 4
 HEAD_TILES = 4
 REST_TILES = M // P - HEAD_TILES
 DIAG_STEP = N + P
-LOAD_PLAN = [4, "B", 4, 8, 8, "head", 12, 12, 12]
-STORE_PLAN = [8, 8, 8, 8, "head", 8, 8, 8, 4]
-STAGE_TILES = 8
+LOAD_PLAN = [4, "B", 8, 16, "head", 32]
+STORE_PLAN = [16, 12, "head", 16, 16]
 AHEAD = 2
 
 
@@ -37,7 +36,7 @@ def tile_modelnew_t_kernel(tc, A, B, grad_out, out):
         resident = ctx.enter_context(tc.tile_pool(name="resident", bufs=1))
         work = ctx.enter_context(tc.tile_pool(name="work", bufs=3))
         quant = ctx.enter_context(tc.tile_pool(name="quant", bufs=AHEAD + 1))
-        staging = ctx.enter_context(tc.tile_pool(name="staging", bufs=6))
+        staging = ctx.enter_context(tc.tile_pool(name="staging", bufs=1))
         tpsum = ctx.enter_context(tc.psum_pool(name="tpsum", bufs=4))
         apsum = ctx.enter_context(tc.psum_pool(name="apsum", bufs=4))
         ctx.enter_context(tc.manual_schedule())
@@ -86,15 +85,6 @@ def tile_modelnew_t_kernel(tc, A, B, grad_out, out):
                 channel_multiplier=1,
             )
 
-        def mask_begin(flat, name):
-            wide = consts.tile([P, HEAD_TILES, P], F32, name=name)
-            nc.vector.tensor_copy(out=wide[:], in_=diagonal(flat))
-            select_lower(wide[:])
-            return wide
-
-        def mask_end(flat, wide):
-            nc.vector.tensor_copy(out=diagonal(flat), in_=wide[:])
-
         def transposes(tiles):
             banks = []
             for j in range(2):
@@ -105,7 +95,7 @@ def tile_modelnew_t_kernel(tc, A, B, grad_out, out):
                         col = (2 * a + u) * P
                         nc.tensor.transpose(
                             out=bank[:, col : col + P],
-                            in_=words[:, u : 2 * P : 2],
+                            in_=words[:, u * P : (u + 1) * P],
                             identity=ident[:],
                         )
                 banks.append(bank)
@@ -166,7 +156,7 @@ def tile_modelnew_t_kernel(tc, A, B, grad_out, out):
         def do_mx(g):
             tiles, s, lo, last = groups[g]
             if lo == 0:
-                stage_of[s] = staging.tile([P, STAGE_TILES, K], F32, name="stage", align_bytes=256)
+                stage_of[s] = staging.tile([P, store_rows[s][1], K], F32, name="stage%d" % s, align_bytes=256)
             stage = stage_of[s]
             codes, scales = quant_of[g]
             for a in range(GROUP):
@@ -207,25 +197,21 @@ def tile_modelnew_t_kernel(tc, A, B, grad_out, out):
                     )
 
         head_at = [g for g in range(n_groups) if groups[g][0] is None][0]
-        wide_of = {}
 
         def flip(g):
             if g + 2 == head_at:
-                wide_of[0] = mask_begin(g_head, "g_diag")
-            if g + 1 == head_at:
-                mask_end(g_head, wide_of[0])
+                select_lower(diagonal(g_head))
             do_t(g)
 
+        select_lower(diagonal(b_sb))
         flip(0)
-        b_wide = mask_begin(b_sb, "b_diag")
         do_c(0)
-        mask_end(b_sb, b_wide)
-        flip(1)
         l_banks = transposes([b_sb[:, t * N : (t + 1) * N] for t in range(HEAD_TILES)])
-        do_c(1)
         l_grouped = regroup(l_banks, consts, "l_grouped")
-        l_codes, l_scales = quantise(l_grouped, consts, "l", E4M3X4)
         do_q(0)
+        l_codes, l_scales = quantise(l_grouped, consts, "l", E4M3X4)
+        flip(1)
+        do_c(1)
         for g in range(2, AHEAD + 1):
             flip(g)
             if g < AHEAD:

@@ -20,7 +20,7 @@ GROUP = 4
 HEAD_TILES = 4
 REST_TILES = M // P - HEAD_TILES
 DIAG_STEP = N + P
-LOAD_PLAN = [4, "B", 8, 16, "head", 32]
+LOAD_PLAN = ["B", 4, 8, 16, "head", 32]
 STORE_PLAN = [16, 12, "head", 16, 16]
 AHEAD = 2
 
@@ -204,24 +204,21 @@ def tile_modelnew_t_kernel(tc, A, B, grad_out, out):
             do_t(g)
 
         select_lower(diagonal(b_sb))
-        flip(0)
-        do_c(0)
         l_banks = transposes([b_sb[:, t * N : (t + 1) * N] for t in range(HEAD_TILES)])
-        l_grouped = regroup(l_banks, consts, "l_grouped")
-        do_q(0)
-        l_codes, l_scales = quantise(l_grouped, consts, "l", E4M3X4)
-        flip(1)
-        do_c(1)
-        for g in range(2, AHEAD + 1):
+        for g in range(AHEAD + 1):
             flip(g)
-            if g < AHEAD:
+            if g == 0:
+                l_grouped = regroup(l_banks, consts, "l_grouped")
+                do_c(0)
+                l_codes, l_scales = quantise(l_grouped, consts, "l", E4M3X4)
+                do_q(0)
+            elif g < AHEAD:
                 do_c(g)
-                do_q(g - 1)
         for g in range(n_groups):
-            if g + AHEAD + 1 < n_groups:
-                flip(g + AHEAD + 1)
             if g + AHEAD < n_groups:
                 do_c(g + AHEAD)
-            if g + AHEAD - 1 < n_groups:
-                do_q(g + AHEAD - 1)
+            if g + 1 < n_groups:
+                do_q(g + 1)
             do_mx(g)
+            if g + AHEAD + 1 < n_groups:
+                flip(g + AHEAD + 1)

@@ -20,8 +20,8 @@ GROUP = 4
 HEAD_TILES = 4
 REST_TILES = M // P - HEAD_TILES
 DIAG_STEP = N + P
-LOAD_PLAN = ["B", 4, 8, 16, "head", 32]
-STORE_PLAN = [16, 12, "head", 16, 16]
+LOAD_PLAN = [4, "B", 8, 16, 32, "head"]
+STORE_PLAN = [12, 12, 12, 12, "head", 12]
 AHEAD = 2
 
 
@@ -46,17 +46,21 @@ def tile_modelnew_t_kernel(tc, A, B, grad_out, out):
         b_sb = resident.tile([P, HEAD_TILES * DIAG_STEP], BF16, name="b_sb", align_bytes=256)
         g_head = resident.tile([P, HEAD_TILES * DIAG_STEP], BF16, name="g_head", align_bytes=256)
 
-        def zero_above(eng, flat):
-            for t in range(HEAD_TILES - 1):
-                eng.memset(flat[:, t * N + (t + 1) * P : (t + 1) * N], 0.0)
-
         def load_lower(dst, src):
-            zero_above(nc.vector, dst)
-            for t in range(HEAD_TILES):
+            for t in range(HEAD_TILES - 1):
+                nc.vector.memset(dst[:, t * N + max(2, t + 1) * P : (t + 1) * N], 0.0)
+            nc.sync.dma_start(
+                out=dst[:, 0 : 2 * N].rearrange("p (t n) -> p t n", n=N)[:, :, 0 : 2 * P],
+                in_=src[0 : 2 * P, 0 : 2 * P].rearrange("(t p) n -> p t n", p=P),
+            )
+            for t in range(2, HEAD_TILES):
                 kept = (t + 1) * P
                 nc.sync.dma_start(
                     out=dst[:, t * N : t * N + kept], in_=src[t * P : (t + 1) * P, 0:kept]
                 )
+
+        def zero_loaded(eng, dst):
+            eng.memset(dst[:, P : 2 * P], 0.0)
 
         rest_tiles = []
         for c, item in enumerate(LOAD_PLAN):
@@ -200,20 +204,21 @@ def tile_modelnew_t_kernel(tc, A, B, grad_out, out):
 
         def flip(g):
             if g + 2 == head_at:
+                zero_loaded(nc.gpsimd, g_head)
                 select_lower(diagonal(g_head))
             do_t(g)
 
         select_lower(diagonal(b_sb))
+        flip(0)
+        do_c(0)
+        do_q(0)
+        zero_loaded(nc.vector, b_sb)
         l_banks = transposes([b_sb[:, t * N : (t + 1) * N] for t in range(HEAD_TILES)])
-        for g in range(AHEAD + 1):
-            flip(g)
-            if g == 0:
-                l_grouped = regroup(l_banks, consts, "l_grouped")
-                do_c(0)
-                l_codes, l_scales = quantise(l_grouped, consts, "l", E4M3X4)
-                do_q(0)
-            elif g < AHEAD:
-                do_c(g)
+        l_grouped = regroup(l_banks, consts, "l_grouped")
+        l_codes, l_scales = quantise(l_grouped, consts, "l", E4M3X4)
+        flip(1)
+        do_c(1)
+        flip(2)
         for g in range(n_groups):
             if g + AHEAD < n_groups:
                 do_c(g + AHEAD)

@@ -196,7 +196,8 @@ def tile_modelnew_t_kernel(tc, A, B, grad_out, out):
                         in_=stage[:, 0:count, :],
                     )
                 else:
-                    nc.sync.dma_start(
+                    queue = nc.scalar if g == n_groups - 1 else nc.sync
+                    queue.dma_start(
                         out=o_rest[:, first_tile : first_tile + count, :], in_=stage[:, 0:count, :]
                     )
 

from contextlib import ExitStack

import concourse.mybir as mybir
from concourse.masks import make_identity

F32 = mybir.dt.float32
BF16 = mybir.dt.bfloat16
U32 = mybir.dt.uint32
U8 = mybir.dt.uint8
E4M3X4 = mybir.dt.float8_e4m3fn_x4
E5M2X4 = mybir.dt.float8_e5m2_x4
IS_GE = mybir.AluOpType.is_ge

P = 128
M, K, N = 8192, 512, 512
FLOPS = 2 * M * K * N
BYTES = M * N * 2 + K * N * 2 + M * K * 4

GROUP = 4
HEAD_TILES = 4
REST_TILES = M // P - HEAD_TILES
DIAG_STEP = N + P
LOAD_PLAN = [4, "B", 8, 16, 32, "head"]
STORE_PLAN = [12, 12, 12, 12, "head", 12]
AHEAD = 2


def diagonal(flat):
    return flat[:, 0 : HEAD_TILES * DIAG_STEP].rearrange("p (t c) -> p t c", c=DIAG_STEP)[:, :, 0:P]


def tile_modelnew_t_kernel(tc, A, B, grad_out, out):
    nc = tc.nc
    with ExitStack() as ctx:
        consts = ctx.enter_context(tc.tile_pool(name="consts", bufs=1))
        resident = ctx.enter_context(tc.tile_pool(name="resident", bufs=1))
        work = ctx.enter_context(tc.tile_pool(name="work", bufs=3))
        quant = ctx.enter_context(tc.tile_pool(name="quant", bufs=AHEAD + 1))
        staging = ctx.enter_context(tc.tile_pool(name="staging", bufs=1))
        tpsum = ctx.enter_context(tc.psum_pool(name="tpsum", bufs=4))
        apsum = ctx.enter_context(tc.psum_pool(name="apsum", bufs=4))
        ctx.enter_context(tc.manual_schedule())

        g_rest = grad_out[HEAD_TILES * P : M, :].rearrange("(p t) n -> p t n", t=REST_TILES)
        o_rest = out[HEAD_TILES * P : M, :].rearrange("(p t) k -> p t k", t=REST_TILES)
        b_sb = resident.tile([P, HEAD_TILES * DIAG_STEP], BF16, name="b_sb", align_bytes=256)
        g_head = resident.tile([P, HEAD_TILES * DIAG_STEP], BF16, name="g_head", align_bytes=256)

        def load_lower(dst, src):
            for t in range(HEAD_TILES - 1):
                nc.vector.memset(dst[:, t * N + max(2, t + 1) * P : (t + 1) * N], 0.0)
            nc.sync.dma_start(
                out=dst[:, 0 : 2 * N].rearrange("p (t n) -> p t n", n=N)[:, :, 0 : 2 * P],
                in_=src[0 : 2 * P, 0 : 2 * P].rearrange("(t p) n -> p t n", p=P),
            )
            for t in range(2, HEAD_TILES):
                kept = (t + 1) * P
                nc.sync.dma_start(
                    out=dst[:, t * N : t * N + kept], in_=src[t * P : (t + 1) * P, 0:kept]
                )

        def zero_loaded(eng, dst):
            eng.memset(dst[:, P : 2 * P], 0.0)

        rest_tiles = []
        for c, item in enumerate(LOAD_PLAN):
            if item == "B":
                load_lower(b_sb, B)
            elif item == "head":
                load_lower(g_head, grad_out[0 : HEAD_TILES * P, :])
            else:
                first = len(rest_tiles)
                chunk = resident.tile([P, item, N], BF16, name="g_chunk%d" % c, align_bytes=256)
                nc.sync.dma_start(out=chunk[:], in_=g_rest[:, first : first + item, :])
                rest_tiles.extend([chunk[:, t, :] for t in range(item)])
        assert len(rest_tiles) == REST_TILES

        ident = consts.tile([P, P], F32, name="ident")
        make_identity(nc, ident[:])

        def select_lower(blocks):
            nc.gpsimd.affine_select(
                out=blocks,
                in_=blocks,
                pattern=[[0, HEAD_TILES], [-1, P]],
                compare_op=IS_GE,
                fill=0.0,
                base=0,
                channel_multiplier=1,
            )

        def transposes(tiles):
            banks = []
            for j in range(2):
                bank = tpsum.tile([P, 512], F32, name="bank")
                for a in range(2):
                    words = tiles[2 * j + a].bitcast(F32)
                    for u in range(2):
                        col = (2 * a + u) * P
                        nc.tensor.transpose(
                            out=bank[:, col : col + P],
                            in_=words[:, u * P : (u + 1) * P],
                            identity=ident[:],
                        )
                banks.append(bank)
            return banks

        def regroup(banks, pool, name):
            grouped = pool.tile([P, GROUP * P * 4], BF16, name=name, align_bytes=64)
            words = grouped[:].bitcast(F32)
            for j in range(2):
                dst = words[:, 512 * j : 512 * (j + 1)].rearrange("p (a m u) -> p a m u", a=2, u=2)
                src = banks[j][:].rearrange("p (a u m) -> p a m u", a=2, u=2)
                if j == 0:
                    nc.vector.tensor_copy(out=dst, in_=src)
                else:
                    nc.scalar.copy(out=dst, in_=src)
            return grouped

        def quantise(grouped, pool, name, fmt):
            codes = pool.tile([P, GROUP * P], U32, name=name + "_codes", align_bytes=64)
            scales = pool.tile([P, GROUP * P], U8, name=name + "_scales", align_bytes=64)
            nc.vector.quantize_mx(out=codes[:].bitcast(fmt), scales=scales[:], in_=grouped[:])
            return codes, scales


        groups = []
        store_rows = []
        first = 0
        for s, item in enumerate(STORE_PLAN):
            if item == "head":
                store_rows.append((None, HEAD_TILES))
                groups.append((None, s, 0, True))
            else:
                store_rows.append((first, item))
                for lo in range(0, item, GROUP):
                    tiles = rest_tiles[first + lo : first + lo + GROUP]
                    groups.append((tiles, s, lo, lo + GROUP == item))
                first += item
        assert first == REST_TILES
        n_groups = len(groups)

        banks_of = {}
        grouped_of = {}
        quant_of = {}
        stage_of = {}

        def do_t(g):
            tiles = groups[g][0]
            if tiles is None:
                tiles = [g_head[:, t * N : (t + 1) * N] for t in range(HEAD_TILES)]
            banks_of[g] = transposes(tiles)

        def do_c(g):
            grouped_of[g] = regroup(banks_of[g], work, "grouped")

        def do_q(g):
            quant_of[g] = quantise(grouped_of[g], quant, "g", E5M2X4)

        def do_mx(g):
            tiles, s, lo, last = groups[g]
            if lo == 0:
                stage_of[s] = staging.tile([P, store_rows[s][1], K], F32, name="stage%d" % s, align_bytes=256)
            stage = stage_of[s]
            codes, scales = quant_of[g]
            for a in range(GROUP):
                acc = apsum.tile([P, K], F32, name="acc")
                nc.tensor.matmul_mx(
                    out=acc[:],
                    lhsT=codes[:, a * P : (a + 1) * P].bitcast(E5M2X4),
                    lhsT_scale=scales[:, a * P : (a + 1) * P],
                    rhs=l_codes[:].bitcast(E4M3X4),
                    rhs_scale=l_scales[:],
                    start=True,
                    stop=True,
                )
                if ((g * GROUP + a) * 1) % 3 < 1:
                    nc.vector.tensor_copy(out=stage[:, lo + a, :], in_=acc[:])
                else:
                    nc.scalar.copy(out=stage[:, lo + a, :], in_=acc[:])
                if tiles is None:
                    nc.gpsimd.affine_select(
                        out=stage[:, a, a * P : K],
                        in_=stage[:, a, a * P : K],
                        pattern=[[-1, K - a * P]],
                        compare_op=IS_GE,
                        fill=0.0,
                        base=0,
                        channel_multiplier=1,
                    )
            if last:
                first_tile, count = store_rows[s]
                if first_tile is None:
                    nc.sync.dma_start(
                        out=out[0 : count * P, :].rearrange("(t p) k -> p t k", p=P),
                        in_=stage[:, 0:count, :],
                    )
                else:
                    queue = nc.scalar if g == n_groups - 1 else nc.sync
                    queue.dma_start(
                        out=o_rest[:, first_tile : first_tile + count, :], in_=stage[:, 0:count, :]
                    )

        head_at = [g for g in range(n_groups) if groups[g][0] is None][0]

        def flip(g):
            if g + 2 == head_at:
                zero_loaded(nc.gpsimd, g_head)
                select_lower(diagonal(g_head))
            do_t(g)

        select_lower(diagonal(b_sb))
        flip(0)
        do_c(0)
        do_q(0)
        zero_loaded(nc.vector, b_sb)
        l_banks = transposes([b_sb[:, t * N : (t + 1) * N] for t in range(HEAD_TILES)])
        l_grouped = regroup(l_banks, consts, "l_grouped")
        l_codes, l_scales = quantise(l_grouped, consts, "l", E4M3X4)
        flip(1)
        do_c(1)
        flip(2)
        for g in range(n_groups):
            if g + AHEAD < n_groups:
                do_c(g + AHEAD)
            if g + 1 < n_groups:
                do_q(g + 1)
            do_mx(g)
            if g + AHEAD + 1 < n_groups:
                flip(g + AHEAD + 1)
